import numpy as np
import ml_dtypes


def mxq(x, axis, fmt="e4m3"):
    dtype, down = {"e4m3": (ml_dtypes.float8_e4m3fn, 7), "e5m2": (ml_dtypes.float8_e5m2, 14)}[fmt]
    v = np.moveaxis(np.asarray(x, np.float32).astype(ml_dtypes.bfloat16).astype(np.float64), axis, -1)
    blocks = v.reshape(v.shape[:-1] + (-1, 32))
    amax = np.abs(blocks).max(-1, keepdims=True)
    byte = np.maximum(np.where(amax > 0, np.frexp(amax)[1] - 1 + 127, 0) - down, 1)
    scale = np.exp2(byte - 127.0)
    codes = (blocks / scale).astype(np.float32).astype(dtype).astype(np.float64)
    return np.moveaxis((codes * scale).reshape(v.shape), -1, axis)


WIDE = False


def mx_kscale(k):
    if not WIDE:
        return np.ones(k)
    levels = np.array([10, -10, 5, -5, 0])
    a = np.random.permutation(np.resize(levels, k // 512 * 4)).reshape(k // 512, 4)
    idx = np.arange(k)
    return np.exp2(a[idx // 512, idx % 128 // 32])


BF16 = ml_dtypes.bfloat16


def bf(x):
    return np.asarray(x, np.float32).astype(BF16)


def f64(x):
    return np.asarray(x).astype(np.float64)


E2M1 = np.array([0.0, 0.5, 1.0, 1.5, 2.0, 3.0, 4.0, 6.0, -0.0, -0.5, -1.0, -1.5, -2.0, -3.0, -4.0, -6.0])


def pack_weight(w, fmt):
    k, n = w.shape
    w = f64(bf(w)).reshape(k // 32, 32, n)
    amax = np.abs(w).max(1)
    if fmt == "e4m3":
        byte = np.frexp(amax)[1] - 1 + 127 - 7
    else:
        mant, ex = np.frexp(amax / 6.0)
        byte = np.where(mant > 0.5, ex, ex - 1) + 127
    byte = np.clip(np.where(amax > 0, byte, 1), 1, 254)
    scaled = (w * np.exp2(127.0 - byte)[:, None, :]).reshape(k, n).astype(np.float32)
    by_word = np.ascontiguousarray(scaled.reshape(k // 512, 128, 4, n).transpose(0, 1, 3, 2))
    if fmt == "e4m3":
        words = by_word.astype(ml_dtypes.float8_e4m3fn).view(np.uint8)
    else:
        c = by_word.astype(ml_dtypes.float4_e2m1fn).view(np.uint8) & 0xF
        words = c[..., 0::2] | (c[..., 1::2] << 4)
    return np.ascontiguousarray(words), np.ascontiguousarray(byte.astype(np.uint8).reshape(k // 512, 16, n))


def unpack_weight(words, scales, fmt):
    g, p, n, _ = words.shape
    if fmt == "e4m3":
        vals = np.ascontiguousarray(words).view(ml_dtypes.float8_e4m3fn).astype(np.float64)
    else:
        nib = np.empty((g, p, n, 4), np.uint8)
        nib[..., 0::2] = words & 0xF
        nib[..., 1::2] = words >> 4
        vals = E2M1[nib]
    vals = vals * np.repeat(np.exp2(scales.astype(np.float64) - 127.0), 8, axis=1)[..., None]
    return vals.transpose(0, 1, 3, 2).reshape(g * 512, n)


B, P, D, NL, T, E, G = 2, 128, 8192, 16, 2, 1, 2
WG = NL * NL * T * G
CLIP = 1.0
LOG_2PI = np.log(2.0 * np.pi)
FMT = "e4m3"


def clip(v):
    return np.clip(v, -CLIP, CLIP)


def gaussian_multi(m1, v1, m2, v2):
    v1s = np.exp(2.0 * v1)
    v2s = np.exp(2.0 * v2)
    add = v1s + v2s
    log_add = np.log(add)
    scale = (-0.5 * (LOG_2PI + log_add + (m1 - m2) ** 2 / add)).sum(-1)
    mu = (m1 * v2s + m2 * v1s) / add
    var = v1 + v2 - 0.5 * log_add
    return scale, mu, var


def setup_inputs():
    s = mx_kscale(D)
    x = bf(np.random.standard_normal((B, P, D)) * s)
    s_weight = bf(np.random.standard_normal((B, P, NL, E)))
    s_mu = bf(clip(np.random.standard_normal((B, P, NL, E, G))))
    s_var = bf(clip(np.random.standard_normal((B, P, NL, E, G))))
    tcm_w_words, tcm_w_scales = pack_weight(np.random.standard_normal((D, WG)) / np.sqrt(D) / s[:, None], FMT)
    tcm_b = bf(np.random.standard_normal(WG) * 0.3)
    tcv_w_words, tcv_w_scales = pack_weight(np.random.standard_normal((D, WG)) / np.sqrt(D) / s[:, None], FMT)
    tcv_b = bf(np.random.standard_normal(WG) * 0.3)
    return {"x": x,
            "s_weight": s_weight,
            "s_mu": s_mu,
            "s_var": s_var,
            "tcm_w_words": tcm_w_words,
            "tcm_w_scales": tcm_w_scales,
            "tcm_b": tcm_b,
            "tcv_w_words": tcv_w_words,
            "tcv_w_scales": tcv_w_scales,
            "tcv_b": tcv_b}


def reference(x, s_weight, s_mu, s_var, tcm_w_words, tcm_w_scales, tcm_b, tcv_w_words, tcv_w_scales, tcv_b):
    xq = mxq(f64(x).reshape(B * P, D), 1, "e4m3")
    t_c_mu = clip(((xq @ unpack_weight(tcm_w_words, tcm_w_scales, FMT)) + f64(tcm_b)).reshape(B, P, NL, NL, T, G))[:, :, :, :, :, None, :]
    t_c_var = clip(((xq @ unpack_weight(tcv_w_words, tcv_w_scales, FMT)) + f64(tcv_b)).reshape(B, P, NL, NL, T, G))[:, :, :, :, :, None, :]
    m1 = f64(s_mu)[:, :, None, :, None, :, :]
    v1 = f64(s_var)[:, :, None, :, None, :, :]
    cs_scale, cs_mu, cs_var = gaussian_multi(m1, v1, t_c_mu, t_c_var)
    cs_scale = cs_scale + f64(s_weight)[:, :, None, :, None, :]
    return cs_scale, cs_mu, cs_var

@@ -1,0 +1,356 @@
+import math
+from contextlib import ExitStack
+
+import concourse.mybir as mybir
+from concourse.masks import make_identity
+
+F32 = mybir.dt.float32
+BF16 = mybir.dt.bfloat16
+I32 = mybir.dt.int32
+U32 = mybir.dt.uint32
+U8 = mybir.dt.uint8
+FP8X4 = mybir.dt.float8_e4m3fn_x4
+ALU = mybir.AluOpType
+ACT = mybir.ActivationFunctionType
+
+P = 128
+PACK = 4
+K_PASS = P * PACK
+ROW_TILES = 2
+K = 8192
+PASSES = K // K_PASS
+N = 1024
+HALF = 512
+HALVES = N // HALF
+JTG = 64
+I_HALF = HALF // JTG
+SHARED = 4
+X_CHUNK = 4
+WIDE_PASSES = 2
+NARROW_PASSES = 2
+TRANSPOSE_BANKS = 4
+CLIP = 1.0
+LOG_2PI = math.log(2.0 * math.pi)
+
+FLOPS = 2 * ROW_TILES * P * K * 2 * N
+
+
+def load_scale_rows(nc, planes, scales, a):
+    for quadrant in range(4):
+        nc.sync.dma_start(
+            out=planes[32 * quadrant : 32 * quadrant + 16, a, :].bitcast(I32),
+            in_=scales[SHARED * a : SHARED * (a + 1), 4 * quadrant : 4 * quadrant + 4, :].bitcast(I32),
+        )
+
+
+def mx_pass(nc, acc, x_codes, x_planes, g, rt, words, planes, cols):
+    rows = slice(rt * P, (rt + 1) * P)
+    nc.tensor.matmul_mx(
+        out=acc[:],
+        lhsT=x_codes[:, g, rows].bitcast(FP8X4),
+        lhsT_scale=x_planes[:, g, rows],
+        rhs=words.bitcast(FP8X4),
+        rhs_scale=planes[4 * (g % SHARED) : P, g // SHARED, cols],
+        start=(g == 0),
+        stop=(g == PASSES - 1),
+    )
+
+
+def by_label(full):
+    return full.rearrange("p (i c) -> p i c", i=I_HALF)
+
+
+def for_every_label(small):
+    return small.unsqueeze(1).to_broadcast([P, I_HALF, small.shape[1]])
+
+
+def pair(full, g):
+    return full.rearrange("p (c g) -> p c g", g=2)[:, :, g]
+
+
+def tile_chainlveg_pa_k_kernel(
+    tc,
+    x,
+    s_weight,
+    s_mu,
+    s_var,
+    tcm_w_words,
+    tcm_w_scales,
+    tcm_b,
+    tcv_w_words,
+    tcv_w_scales,
+    tcv_b,
+    out_0,
+    out_1,
+    out_2,
+):
+    nc = tc.nc
+    row_tiles = range(ROW_TILES)
+    halves = range(HALVES)
+    with ExitStack() as ctx:
+        ctx.enter_context(tc.manual_schedule())
+        keep = ctx.enter_context(tc.tile_pool(name="keep", bufs=1))
+        stage = ctx.enter_context(tc.tile_pool(name="stage", bufs=3))
+        wide = ctx.enter_context(tc.tile_pool(name="wide", bufs=5))
+        narrow = ctx.enter_context(tc.tile_pool(name="narrow", bufs=8))
+        psum = ctx.enter_context(tc.psum_pool(name="psum", bufs=1))
+
+        bias_row = keep.tile([P, 2, N], BF16)
+        nc.vector.memset(bias_row[:].rearrange("p w n -> p (w n)").bitcast(I32), 0)
+        planes_v = keep.tile([P, PASSES // SHARED, N], U8, align_bytes=64)
+        planes_m = keep.tile([P, PASSES // SHARED, N], U8, align_bytes=64)
+        nc.vector.memset(planes_v[:].rearrange("p a n -> p (a n)").bitcast(I32), 0)
+        nc.vector.memset(planes_m[:].rearrange("p a n -> p (a n)").bitcast(I32), 0)
+        ones = keep.tile([P, P], BF16)
+        nc.vector.memset(ones[:], 1.0)
+        ident = keep.tile([P, P], F32)
+        make_identity(nc, ident[:])
+
+        x_by_row = x.rearrange("b p k -> p b k")
+        x_raw = []
+        for c in range(PASSES // X_CHUNK):
+            chunk = keep.tile([P, ROW_TILES, X_CHUNK * K_PASS], BF16, name="x_raw%d" % c)
+            nc.sync.dma_start(
+                out=chunk[:],
+                in_=x_by_row[:, :, c * X_CHUNK * K_PASS : (c + 1) * X_CHUNK * K_PASS],
+            )
+            x_raw.append(chunk)
+
+        nc.gpsimd.dma_start(out=bias_row[0:1, 0, :], in_=tcv_b.rearrange("(o n) -> o n", o=1))
+        nc.gpsimd.dma_start(out=bias_row[0:1, 1, :], in_=tcm_b.rearrange("(o n) -> o n", o=1))
+        var_raw = keep.tile([P, ROW_TILES, 32], BF16)
+        mu_raw = keep.tile([P, ROW_TILES, 32], BF16)
+        weight_raw = keep.tile([P, ROW_TILES, 16], BF16)
+        nc.gpsimd.dma_start(out=var_raw[:], in_=s_var.rearrange("b p j e g -> p b (j e g)"))
+        nc.gpsimd.dma_start(out=mu_raw[:], in_=s_mu.rearrange("b p j e g -> p b (j e g)"))
+        nc.gpsimd.dma_start(out=weight_raw[:], in_=s_weight.rearrange("b p j e -> p b (j e)"))
+
+        x_codes = keep.tile([P, PASSES, ROW_TILES * P], U32, align_bytes=64)
+        x_planes = keep.tile([P, PASSES, ROW_TILES * P], U8, align_bytes=64)
+
+        def quantise(g, grouped):
+            nc.vector.quantize_mx(
+                out=x_codes[:, g, :].bitcast(FP8X4), scales=x_planes[:, g, :], in_=grouped[:]
+            )
+
+        waiting = None
+        for g in range(PASSES):
+            c, g_in_chunk = divmod(g, X_CHUNK)
+            flipped = psum.tile(
+                [P, ROW_TILES, 2, P], F32, name="flipped", tag="bank%d" % (g % TRANSPOSE_BANKS)
+            )
+            for rt in row_tiles:
+                words = x_raw[c][:, rt, :].bitcast(F32)
+                first = g_in_chunk * (K_PASS // 2)
+                for u in range(2):
+                    nc.tensor.transpose(
+                        flipped[:, rt, u, :],
+                        words[:, first + u : first + K_PASS // 2 : 2],
+                        ident[:],
+                    )
+            grouped = stage.tile([P, ROW_TILES * P * PACK], BF16, align_bytes=64)
+            copy_out = nc.vector.tensor_copy if g % 4 == 3 else nc.scalar.copy
+            copy_out(
+                out=grouped[:].bitcast(F32).rearrange("p (a r u) -> p a r u", a=ROW_TILES, u=2),
+                in_=flipped[:].rearrange("p a u r -> p a r u"),
+            )
+            if waiting is not None:
+                quantise(g - 1, waiting)
+            waiting = grouped
+        quantise(PASSES - 1, waiting)
+
+        bias_all = keep.tile([P, 2, N], F32)
+        for w in range(2):
+            for h in halves:
+                cols = slice(h * HALF, (h + 1) * HALF)
+                spread = psum.tile([P, HALF], F32, name="spread", tag="bank%d" % (4 + 2 * w + h))
+                nc.tensor.matmul(
+                    out=spread[:], lhsT=ones[:], rhs=bias_row[:, w, cols], start=True, stop=True
+                )
+                nc.scalar.copy(out=bias_all[:, w, cols], in_=spread[:])
+
+        m1 = keep.tile([P, ROW_TILES, JTG], F32)
+        v1 = keep.tile([P, ROW_TILES, JTG], F32)
+        for table, raw in ((v1, var_raw), (m1, mu_raw)):
+            nc.vector.tensor_copy(
+                out=table[:].rearrange("p b (j t g) -> p (b j) t g", t=2, g=2),
+                in_=raw[:]
+                .rearrange("p b (j g) -> p (b j) g", g=2)
+                .unsqueeze(2)
+                .to_broadcast([P, ROW_TILES * 16, 2, 2]),
+            )
+        inv_e1 = keep.tile([P, ROW_TILES, JTG], F32)
+        nc.scalar.activation(out=inv_e1[:], in_=v1[:], func=ACT.Exp, scale=-2.0)
+        var_pairs = var_raw[:].rearrange("p b (j g) -> p (b j) g", g=2)
+        base_j = keep.tile([P, ROW_TILES * 16], F32)
+        nc.vector.tensor_tensor(
+            out=base_j[:], in0=var_pairs[:, :, 0], in1=var_pairs[:, :, 1], op=ALU.add
+        )
+        nc.vector.tensor_tensor(
+            out=base_j[:], in0=weight_raw[:].rearrange("p b j -> p (b j)"), in1=base_j[:], op=ALU.subtract
+        )
+        base = keep.tile([P, ROW_TILES, JTG // 2], F32)
+        nc.vector.tensor_scalar(
+            out=base[:].rearrange("p b (j t) -> p (b j) t", t=2),
+            in0=base_j[:].unsqueeze(2).to_broadcast([P, ROW_TILES * 16, 2]),
+            scalar1=-LOG_2PI,
+            scalar2=None,
+            op0=ALU.add,
+        )
+
+        acc_v = [
+            [psum.tile([P, HALF], F32, name="acc_v", tag="bank%d" % (2 * rt + h)) for h in halves]
+            for rt in row_tiles
+        ]
+        for first in range(0, PASSES, WIDE_PASSES):
+            if first % SHARED == 0:
+                load_scale_rows(nc, planes_v, tcv_w_scales, first // SHARED)
+            w_words = wide.tile([P, WIDE_PASSES, N], U32, align_bytes=64)
+            nc.sync.dma_start(
+                out=w_words[:].bitcast(I32),
+                in_=tcv_w_words[first : first + WIDE_PASSES]
+                .rearrange("g p n t -> p g (n t)")
+                .bitcast(I32),
+            )
+            for g in range(first, first + WIDE_PASSES):
+                for rt in row_tiles:
+                    for h in halves:
+                        cols = slice(h * HALF, (h + 1) * HALF)
+                        mx_pass(
+                            nc, acc_v[rt][h], x_codes, x_planes, g, rt,
+                            w_words[:, g - first, cols], planes_v, cols,
+                        )
+
+        acc_m = [
+            [psum.tile([P, HALF], F32, name="acc_m", tag="bank%d" % (4 + 2 * h + rt)) for h in halves]
+            for rt in row_tiles
+        ]
+        for h in halves:
+            cols = slice(h * HALF, (h + 1) * HALF)
+            for first in range(0, PASSES, NARROW_PASSES):
+                if h == 0 and first % SHARED == 0:
+                    load_scale_rows(nc, planes_m, tcm_w_scales, first // SHARED)
+                w_words = narrow.tile([P, NARROW_PASSES, HALF], U32, align_bytes=64)
+                nc.sync.dma_start(
+                    out=w_words[:].bitcast(I32),
+                    in_=tcm_w_words[first : first + NARROW_PASSES, :, cols, :]
+                    .rearrange("g p n t -> p g (n t)")
+                    .bitcast(I32),
+                )
+                for g in range(first, first + NARROW_PASSES):
+                    for rt in row_tiles:
+                        mx_pass(
+                            nc, acc_m[rt][h], x_codes, x_planes, g, rt,
+                            w_words[:, g - first, :], planes_m, cols,
+                        )
+
+        blocks = [(h, rt) for h in halves for rt in row_tiles]
+        v2 = {}
+        s = {}
+        for h, rt in blocks:
+            v2[h, rt] = keep.tile([P, HALF], F32, name="v2_%d%d" % (h, rt))
+            s[h, rt] = keep.tile([P, HALF], F32, name="s_%d%d" % (h, rt))
+        for h in halves:
+            cols = slice(h * HALF, (h + 1) * HALF)
+            for rt in row_tiles:
+                nc.vector.tensor_tensor(
+                    out=v2[h, rt][:], in0=acc_v[rt][h][:], in1=bias_all[:, 0, cols], op=ALU.add
+                )
+            for rt in row_tiles:
+                nc.vector.tensor_scalar(
+                    out=v2[h, rt][:], in0=v2[h, rt][:],
+                    scalar1=-CLIP, scalar2=CLIP, op0=ALU.max, op1=ALU.min,
+                )
+            for rt in row_tiles:
+                nc.vector.tensor_tensor(
+                    out=by_label(s[h, rt][:]), in0=by_label(v2[h, rt][:]),
+                    in1=for_every_label(v1[:, rt, :]), op=ALU.subtract,
+                )
+            for rt in row_tiles:
+                nc.scalar.activation(out=s[h, rt][:], in_=s[h, rt][:], func=ACT.Sigmoid, scale=-2.0)
+        log_s = [keep.tile([P, HALVES, HALF], F32, name="log_s%d" % rt) for rt in row_tiles]
+        for h, rt in blocks:
+            nc.scalar.activation(out=log_s[rt][:, h, :], in_=s[h, rt][:], func=ACT.Ln)
+        inv_add = {}
+        for h, rt in blocks:
+            inv_add[h, rt] = keep.tile([P, HALF], F32, name="inv_add_%d%d" % (h, rt))
+            nc.vector.tensor_tensor(
+                out=by_label(inv_add[h, rt][:]), in0=by_label(s[h, rt][:]),
+                in1=for_every_label(inv_e1[:, rt, :]), op=ALU.mult,
+            )
+        part = {}
+        for h, rt in blocks:
+            part[h, rt] = keep.tile([P, HALF // 2], F32, name="part_%d%d" % (h, rt))
+            nc.vector.tensor_tensor(
+                out=part[h, rt][:], in0=pair(log_s[rt][:, h, :], 0), in1=pair(log_s[rt][:, h, :], 1),
+                op=ALU.add,
+            )
+        for h, rt in blocks:
+            nc.vector.scalar_tensor_tensor(
+                out=by_label(part[h, rt][:]), in0=by_label(part[h, rt][:]), scalar=0.5,
+                in1=for_every_label(base[:, rt, :]), op0=ALU.mult, op1=ALU.add,
+            )
+        for h, rt in blocks:
+            nc.vector.scalar_tensor_tensor(
+                out=log_s[rt][:, h, :], in0=log_s[rt][:, h, :], scalar=0.5,
+                in1=v2[h, rt][:], op0=ALU.mult, op1=ALU.add,
+            )
+        for rt in row_tiles:
+            nc.sync.dma_start(
+                out=out_2[rt].rearrange("p i j t e g -> p (i j t e g)"),
+                in_=log_s[rt][:].rearrange("p h n -> p (h n)"),
+            )
+
+        for h in halves:
+            cols = slice(h * HALF, (h + 1) * HALF)
+            diff = [keep.tile([P, HALF], F32, name="diff_%d%d" % (h, rt)) for rt in row_tiles]
+            square = [keep.tile([P, HALF], F32, name="square_%d%d" % (h, rt)) for rt in row_tiles]
+            mean = [keep.tile([P, HALF], F32, name="mean_%d%d" % (h, rt)) for rt in row_tiles]
+            scale = [keep.tile([P, HALF // 2], F32, name="scale_%d%d" % (h, rt)) for rt in row_tiles]
+            for rt in row_tiles:
+                nc.vector.tensor_tensor(
+                    out=diff[rt][:], in0=acc_m[rt][h][:], in1=bias_all[:, 1, cols], op=ALU.add
+                )
+            for rt in row_tiles:
+                nc.vector.tensor_scalar(
+                    out=diff[rt][:], in0=diff[rt][:],
+                    scalar1=-CLIP, scalar2=CLIP, op0=ALU.max, op1=ALU.min,
+                )
+            for rt in row_tiles:
+                nc.vector.tensor_tensor(
+                    out=by_label(diff[rt][:]), in0=by_label(diff[rt][:]),
+                    in1=for_every_label(m1[:, rt, :]), op=ALU.subtract,
+                )
+            for rt in row_tiles:
+                nc.scalar.activation(out=square[rt][:], in_=diff[rt][:], func=ACT.Square)
+            for rt in row_tiles:
+                nc.vector.tensor_tensor(
+                    out=mean[rt][:], in0=diff[rt][:], in1=s[h, rt][:], op=ALU.mult
+                )
+            for rt in row_tiles:
+                nc.vector.tensor_tensor(
+                    out=by_label(mean[rt][:]), in0=by_label(mean[rt][:]),
+                    in1=for_every_label(m1[:, rt, :]), op=ALU.add,
+                )
+                nc.sync.dma_start(
+                    out=out_1[rt].rearrange("p i j t e g -> p (i j t e g)")[:, cols], in_=mean[rt][:]
+                )
+            for rt in row_tiles:
+                nc.vector.tensor_tensor(
+                    out=square[rt][:], in0=square[rt][:], in1=inv_add[h, rt][:], op=ALU.mult
+                )
+            for rt in row_tiles:
+                nc.vector.tensor_tensor(
+                    out=scale[rt][:], in0=pair(square[rt][:], 0), in1=pair(square[rt][:], 1), op=ALU.add
+                )
+            for rt in row_tiles:
+                nc.vector.scalar_tensor_tensor(
+                    out=scale[rt][:], in0=scale[rt][:], scalar=-0.5,
+                    in1=part[h, rt][:], op0=ALU.mult, op1=ALU.add,
+                )
+                nc.sync.dma_start(
+                    out=out_0[rt].rearrange("p i j t e -> p (i j t e)")[
+                        :, h * (HALF // 2) : (h + 1) * (HALF // 2)
+                    ],
+                    in_=scale[rt][:],
+                )

@@ -37,9 +37,9 @@ FLOPS = 2 * ROW_TILES * P * K * 2 * N
 
 def load_scale_rows(nc, planes, scales, a):
     for quadrant in range(4):
-        nc.sync.dma_start(
-            out=planes[32 * quadrant : 32 * quadrant + 16, a, :].bitcast(I32),
-            in_=scales[SHARED * a : SHARED * (a + 1), 4 * quadrant : 4 * quadrant + 4, :].bitcast(I32),
+        nc.gpsimd.dma_start(
+            out=planes[32 * quadrant : 32 * quadrant + 16, a, :].bitcast(F32),
+            in_=scales[SHARED * a : SHARED * (a + 1), 4 * quadrant : 4 * quadrant + 4, :].bitcast(F32),
         )
 
 

@@ -20,48 +20,35 @@ ROW_TILES = 2
 K = 8192
 PASSES = K // K_PASS
 N = 1024
-HALF = 512
-HALVES = N // HALF
+BANK = 512
+BANKS = 8
 JTG = 64
-I_HALF = HALF // JTG
 SHARED = 4
 X_CHUNK = 4
-WIDE_PASSES = 2
-NARROW_PASSES = 2
+LOAD_WORDS = 1024
 TRANSPOSE_BANKS = 4
 CLIP = 1.0
 LOG_2PI = math.log(2.0 * math.pi)
+
+ROUNDS = (("v", 0, 512), ("v", 512, 512), ("m", 0, 512), ("m", 512, 256), ("m", 768, 256))
 
 FLOPS = 2 * ROW_TILES * P * K * 2 * N
 
 
 def load_scale_rows(nc, planes, scales, a):
     for quadrant in range(4):
-        nc.gpsimd.dma_start(
-            out=planes[32 * quadrant : 32 * quadrant + 16, a, :].bitcast(F32),
-            in_=scales[SHARED * a : SHARED * (a + 1), 4 * quadrant : 4 * quadrant + 4, :].bitcast(F32),
+        nc.sync.dma_start(
+            out=planes[32 * quadrant : 32 * quadrant + 16, a, :].bitcast(I32),
+            in_=scales[SHARED * a : SHARED * (a + 1), 4 * quadrant : 4 * quadrant + 4, :].bitcast(I32),
         )
 
 
-def mx_pass(nc, acc, x_codes, x_planes, g, rt, words, planes, cols):
-    rows = slice(rt * P, (rt + 1) * P)
-    nc.tensor.matmul_mx(
-        out=acc[:],
-        lhsT=x_codes[:, g, rows].bitcast(FP8X4),
-        lhsT_scale=x_planes[:, g, rows],
-        rhs=words.bitcast(FP8X4),
-        rhs_scale=planes[4 * (g % SHARED) : P, g // SHARED, cols],
-        start=(g == 0),
-        stop=(g == PASSES - 1),
-    )
+def by_label(full, labels):
+    return full.rearrange("p (i c) -> p i c", i=labels)
 
 
-def by_label(full):
-    return full.rearrange("p (i c) -> p i c", i=I_HALF)
-
-
-def for_every_label(small):
-    return small.unsqueeze(1).to_broadcast([P, I_HALF, small.shape[1]])
+def for_every_label(small, labels):
+    return small.unsqueeze(1).to_broadcast([P, labels, small.shape[1]])
 
 
 def pair(full, g):
@@ -86,23 +73,23 @@ def tile_chainlveg_pa_k_kernel(
 ):
     nc = tc.nc
     row_tiles = range(ROW_TILES)
-    halves = range(HALVES)
     with ExitStack() as ctx:
         ctx.enter_context(tc.manual_schedule())
         keep = ctx.enter_context(tc.tile_pool(name="keep", bufs=1))
         stage = ctx.enter_context(tc.tile_pool(name="stage", bufs=3))
-        wide = ctx.enter_context(tc.tile_pool(name="wide", bufs=5))
-        narrow = ctx.enter_context(tc.tile_pool(name="narrow", bufs=8))
+        ring = ctx.enter_context(tc.tile_pool(name="ring", bufs=10))
         psum = ctx.enter_context(tc.psum_pool(name="psum", bufs=1))
 
         bias_row = keep.tile([P, 2, N], BF16)
         nc.vector.memset(bias_row[:].rearrange("p w n -> p (w n)").bitcast(I32), 0)
-        planes_v = keep.tile([P, PASSES // SHARED, N], U8, align_bytes=64)
-        planes_m = keep.tile([P, PASSES // SHARED, N], U8, align_bytes=64)
-        nc.vector.memset(planes_v[:].rearrange("p a n -> p (a n)").bitcast(I32), 0)
-        nc.vector.memset(planes_m[:].rearrange("p a n -> p (a n)").bitcast(I32), 0)
         ones = keep.tile([P, P], BF16)
         nc.vector.memset(ones[:], 1.0)
+        planes = {}
+        for name in ("v", "m"):
+            planes[name] = keep.tile(
+                [P, PASSES // SHARED, N], U8, align_bytes=64, name="planes_%s" % name
+            )
+            nc.vector.memset(planes[name][:].rearrange("p a n -> p (a n)").bitcast(I32), 0)
         ident = keep.tile([P, P], F32)
         make_identity(nc, ident[:])
 
@@ -116,14 +103,26 @@ def tile_chainlveg_pa_k_kernel(
             )
             x_raw.append(chunk)
 
-        nc.gpsimd.dma_start(out=bias_row[0:1, 0, :], in_=tcv_b.rearrange("(o n) -> o n", o=1))
-        nc.gpsimd.dma_start(out=bias_row[0:1, 1, :], in_=tcm_b.rearrange("(o n) -> o n", o=1))
+        nc.scalar.dma_start(out=bias_row[0:1, 0, :], in_=tcv_b.rearrange("(o n) -> o n", o=1))
+        nc.scalar.dma_start(out=bias_row[0:1, 1, :], in_=tcm_b.rearrange("(o n) -> o n", o=1))
         var_raw = keep.tile([P, ROW_TILES, 32], BF16)
         mu_raw = keep.tile([P, ROW_TILES, 32], BF16)
         weight_raw = keep.tile([P, ROW_TILES, 16], BF16)
         nc.gpsimd.dma_start(out=var_raw[:], in_=s_var.rearrange("b p j e g -> p b (j e g)"))
         nc.gpsimd.dma_start(out=mu_raw[:], in_=s_mu.rearrange("b p j e g -> p b (j e g)"))
         nc.gpsimd.dma_start(out=weight_raw[:], in_=s_weight.rearrange("b p j e -> p b (j e)"))
+
+        bias_all = keep.tile([P, 2, N], F32)
+        for w in range(2):
+            for h in range(N // BANK):
+                cols = slice(h * BANK, (h + 1) * BANK)
+                spread = psum.tile(
+                    [P, BANK], F32, name="spread", tag="bank%d" % (TRANSPOSE_BANKS + 2 * w + h)
+                )
+                nc.tensor.matmul(
+                    out=spread[:], lhsT=ones[:], rhs=bias_row[:, w, cols], start=True, stop=True
+                )
+                nc.scalar.copy(out=bias_all[:, w, cols], in_=spread[:])
 
         x_codes = keep.tile([P, PASSES, ROW_TILES * P], U32, align_bytes=64)
         x_planes = keep.tile([P, PASSES, ROW_TILES * P], U8, align_bytes=64)
@@ -159,16 +158,6 @@ def tile_chainlveg_pa_k_kernel(
             waiting = grouped
         quantise(PASSES - 1, waiting)
 
-        bias_all = keep.tile([P, 2, N], F32)
-        for w in range(2):
-            for h in halves:
-                cols = slice(h * HALF, (h + 1) * HALF)
-                spread = psum.tile([P, HALF], F32, name="spread", tag="bank%d" % (4 + 2 * w + h))
-                nc.tensor.matmul(
-                    out=spread[:], lhsT=ones[:], rhs=bias_row[:, w, cols], start=True, stop=True
-                )
-                nc.scalar.copy(out=bias_all[:, w, cols], in_=spread[:])
-
         m1 = keep.tile([P, ROW_TILES, JTG], F32)
         v1 = keep.tile([P, ROW_TILES, JTG], F32)
         for table, raw in ((v1, var_raw), (m1, mu_raw)):
@@ -198,159 +187,162 @@ def tile_chainlveg_pa_k_kernel(
             op0=ALU.add,
         )
 
-        acc_v = [
-            [psum.tile([P, HALF], F32, name="acc_v", tag="bank%d" % (2 * rt + h)) for h in halves]
-            for rt in row_tiles
-        ]
-        for first in range(0, PASSES, WIDE_PASSES):
-            if first % SHARED == 0:
-                load_scale_rows(nc, planes_v, tcv_w_scales, first // SHARED)
-            w_words = wide.tile([P, WIDE_PASSES, N], U32, align_bytes=64)
-            nc.sync.dma_start(
-                out=w_words[:].bitcast(I32),
-                in_=tcv_w_words[first : first + WIDE_PASSES]
-                .rearrange("g p n t -> p g (n t)")
-                .bitcast(I32),
-            )
-            for g in range(first, first + WIDE_PASSES):
-                for rt in row_tiles:
-                    for h in halves:
-                        cols = slice(h * HALF, (h + 1) * HALF)
-                        mx_pass(
-                            nc, acc_v[rt][h], x_codes, x_planes, g, rt,
-                            w_words[:, g - first, cols], planes_v, cols,
-                        )
+        weights = {"v": (tcv_w_words, tcv_w_scales), "m": (tcm_w_words, tcm_w_scales)}
 
-        acc_m = [
-            [psum.tile([P, HALF], F32, name="acc_m", tag="bank%d" % (4 + 2 * h + rt)) for h in halves]
-            for rt in row_tiles
-        ]
-        for h in halves:
-            cols = slice(h * HALF, (h + 1) * HALF)
-            for first in range(0, PASSES, NARROW_PASSES):
-                if h == 0 and first % SHARED == 0:
-                    load_scale_rows(nc, planes_m, tcm_w_scales, first // SHARED)
-                w_words = narrow.tile([P, NARROW_PASSES, HALF], U32, align_bytes=64)
+        def multiply(r):
+            name, col0, width = ROUNDS[r]
+            w_words_dram, w_scales_dram = weights[name]
+            cols = slice(col0, col0 + width)
+            acc = [
+                psum.tile([P, width], F32, name="acc", tag="bank%d" % ((2 * r + rt) % BANKS))
+                for rt in row_tiles
+            ]
+            per_load = LOAD_WORDS // width
+            for first in range(0, PASSES, per_load):
+                if col0 == 0 and first % SHARED == 0:
+                    load_scale_rows(nc, planes[name], w_scales_dram, first // SHARED)
+                w_words = ring.tile([P, per_load, width], U32, align_bytes=64, tag="w_words")
                 nc.sync.dma_start(
                     out=w_words[:].bitcast(I32),
-                    in_=tcm_w_words[first : first + NARROW_PASSES, :, cols, :]
+                    in_=w_words_dram[first : first + per_load, :, cols, :]
                     .rearrange("g p n t -> p g (n t)")
                     .bitcast(I32),
                 )
-                for g in range(first, first + NARROW_PASSES):
+                for g in range(first, first + per_load):
                     for rt in row_tiles:
-                        mx_pass(
-                            nc, acc_m[rt][h], x_codes, x_planes, g, rt,
-                            w_words[:, g - first, :], planes_m, cols,
+                        rows = slice(rt * P, (rt + 1) * P)
+                        nc.tensor.matmul_mx(
+                            out=acc[rt][:],
+                            lhsT=x_codes[:, g, rows].bitcast(FP8X4),
+                            lhsT_scale=x_planes[:, g, rows],
+                            rhs=w_words[:, g - first, :].bitcast(FP8X4),
+                            rhs_scale=planes[name][4 * (g % SHARED) : P, g // SHARED, cols],
+                            start=(g == 0),
+                            stop=(g == PASSES - 1),
                         )
+            return acc
 
-        blocks = [(h, rt) for h in halves for rt in row_tiles]
-        v2 = {}
-        s = {}
-        for h, rt in blocks:
-            v2[h, rt] = keep.tile([P, HALF], F32, name="v2_%d%d" % (h, rt))
-            s[h, rt] = keep.tile([P, HALF], F32, name="s_%d%d" % (h, rt))
-        for h in halves:
-            cols = slice(h * HALF, (h + 1) * HALF)
+        v2 = [keep.tile([P, N], F32, name="v2_%d" % rt) for rt in row_tiles]
+        s = [keep.tile([P, N], F32, name="s_%d" % rt) for rt in row_tiles]
+        log_s = [keep.tile([P, N], F32, name="log_s_%d" % rt) for rt in row_tiles]
+        inv_add = [keep.tile([P, N], F32, name="inv_add_%d" % rt) for rt in row_tiles]
+        part = [keep.tile([P, N // 2], F32, name="part_%d" % rt) for rt in row_tiles]
+        diff = [keep.tile([P, N], F32, name="diff_%d" % rt) for rt in row_tiles]
+        square = [keep.tile([P, N], F32, name="square_%d" % rt) for rt in row_tiles]
+        mean = [keep.tile([P, N], F32, name="mean_%d" % rt) for rt in row_tiles]
+        scale = [keep.tile([P, N // 2], F32, name="scale_%d" % rt) for rt in row_tiles]
+
+        def add_bias_and_clip(dst, acc, w, cols):
             for rt in row_tiles:
                 nc.vector.tensor_tensor(
-                    out=v2[h, rt][:], in0=acc_v[rt][h][:], in1=bias_all[:, 0, cols], op=ALU.add
+                    out=dst[rt][:, cols], in0=acc[rt][:], in1=bias_all[:, w, cols], op=ALU.add
                 )
             for rt in row_tiles:
                 nc.vector.tensor_scalar(
-                    out=v2[h, rt][:], in0=v2[h, rt][:],
+                    out=dst[rt][:, cols], in0=dst[rt][:, cols],
                     scalar1=-CLIP, scalar2=CLIP, op0=ALU.max, op1=ALU.min,
                 )
-            for rt in row_tiles:
-                nc.vector.tensor_tensor(
-                    out=by_label(s[h, rt][:]), in0=by_label(v2[h, rt][:]),
-                    in1=for_every_label(v1[:, rt, :]), op=ALU.subtract,
-                )
-            for rt in row_tiles:
-                nc.scalar.activation(out=s[h, rt][:], in_=s[h, rt][:], func=ACT.Sigmoid, scale=-2.0)
-        log_s = [keep.tile([P, HALVES, HALF], F32, name="log_s%d" % rt) for rt in row_tiles]
-        for h, rt in blocks:
-            nc.scalar.activation(out=log_s[rt][:, h, :], in_=s[h, rt][:], func=ACT.Ln)
-        inv_add = {}
-        for h, rt in blocks:
-            inv_add[h, rt] = keep.tile([P, HALF], F32, name="inv_add_%d%d" % (h, rt))
-            nc.vector.tensor_tensor(
-                out=by_label(inv_add[h, rt][:]), in0=by_label(s[h, rt][:]),
-                in1=for_every_label(inv_e1[:, rt, :]), op=ALU.mult,
-            )
-        part = {}
-        for h, rt in blocks:
-            part[h, rt] = keep.tile([P, HALF // 2], F32, name="part_%d%d" % (h, rt))
-            nc.vector.tensor_tensor(
-                out=part[h, rt][:], in0=pair(log_s[rt][:, h, :], 0), in1=pair(log_s[rt][:, h, :], 1),
-                op=ALU.add,
-            )
-        for h, rt in blocks:
-            nc.vector.scalar_tensor_tensor(
-                out=by_label(part[h, rt][:]), in0=by_label(part[h, rt][:]), scalar=0.5,
-                in1=for_every_label(base[:, rt, :]), op0=ALU.mult, op1=ALU.add,
-            )
-        for h, rt in blocks:
-            nc.vector.scalar_tensor_tensor(
-                out=log_s[rt][:, h, :], in0=log_s[rt][:, h, :], scalar=0.5,
-                in1=v2[h, rt][:], op0=ALU.mult, op1=ALU.add,
-            )
-        for rt in row_tiles:
-            nc.sync.dma_start(
-                out=out_2[rt].rearrange("p i j t e g -> p (i j t e g)"),
-                in_=log_s[rt][:].rearrange("p h n -> p (h n)"),
-            )
 
-        for h in halves:
-            cols = slice(h * HALF, (h + 1) * HALF)
-            diff = [keep.tile([P, HALF], F32, name="diff_%d%d" % (h, rt)) for rt in row_tiles]
-            square = [keep.tile([P, HALF], F32, name="square_%d%d" % (h, rt)) for rt in row_tiles]
-            mean = [keep.tile([P, HALF], F32, name="mean_%d%d" % (h, rt)) for rt in row_tiles]
-            scale = [keep.tile([P, HALF // 2], F32, name="scale_%d%d" % (h, rt)) for rt in row_tiles]
+        def after_log_std(acc, col0, width):
+            cols = slice(col0, col0 + width)
+            halved = slice(col0 // 2, (col0 + width) // 2)
+            labels = width // JTG
+            stores = []
+            add_bias_and_clip(v2, acc, 0, cols)
             for rt in row_tiles:
                 nc.vector.tensor_tensor(
-                    out=diff[rt][:], in0=acc_m[rt][h][:], in1=bias_all[:, 1, cols], op=ALU.add
+                    out=by_label(s[rt][:, cols], labels), in0=by_label(v2[rt][:, cols], labels),
+                    in1=for_every_label(v1[:, rt, :], labels), op=ALU.subtract,
                 )
             for rt in row_tiles:
-                nc.vector.tensor_scalar(
-                    out=diff[rt][:], in0=diff[rt][:],
-                    scalar1=-CLIP, scalar2=CLIP, op0=ALU.max, op1=ALU.min,
+                nc.scalar.activation(
+                    out=s[rt][:, cols], in_=s[rt][:, cols], func=ACT.Sigmoid, scale=-2.0
                 )
+            for rt in row_tiles:
+                nc.scalar.activation(out=log_s[rt][:, cols], in_=s[rt][:, cols], func=ACT.Ln)
             for rt in row_tiles:
                 nc.vector.tensor_tensor(
-                    out=by_label(diff[rt][:]), in0=by_label(diff[rt][:]),
-                    in1=for_every_label(m1[:, rt, :]), op=ALU.subtract,
-                )
-            for rt in row_tiles:
-                nc.scalar.activation(out=square[rt][:], in_=diff[rt][:], func=ACT.Square)
-            for rt in row_tiles:
-                nc.vector.tensor_tensor(
-                    out=mean[rt][:], in0=diff[rt][:], in1=s[h, rt][:], op=ALU.mult
+                    out=by_label(inv_add[rt][:, cols], labels), in0=by_label(s[rt][:, cols], labels),
+                    in1=for_every_label(inv_e1[:, rt, :], labels), op=ALU.mult,
                 )
             for rt in row_tiles:
                 nc.vector.tensor_tensor(
-                    out=by_label(mean[rt][:]), in0=by_label(mean[rt][:]),
-                    in1=for_every_label(m1[:, rt, :]), op=ALU.add,
-                )
-                nc.sync.dma_start(
-                    out=out_1[rt].rearrange("p i j t e g -> p (i j t e g)")[:, cols], in_=mean[rt][:]
-                )
-            for rt in row_tiles:
-                nc.vector.tensor_tensor(
-                    out=square[rt][:], in0=square[rt][:], in1=inv_add[h, rt][:], op=ALU.mult
-                )
-            for rt in row_tiles:
-                nc.vector.tensor_tensor(
-                    out=scale[rt][:], in0=pair(square[rt][:], 0), in1=pair(square[rt][:], 1), op=ALU.add
+                    out=part[rt][:, halved], in0=pair(log_s[rt][:, cols], 0),
+                    in1=pair(log_s[rt][:, cols], 1), op=ALU.add,
                 )
             for rt in row_tiles:
                 nc.vector.scalar_tensor_tensor(
-                    out=scale[rt][:], in0=scale[rt][:], scalar=-0.5,
-                    in1=part[h, rt][:], op0=ALU.mult, op1=ALU.add,
+                    out=by_label(part[rt][:, halved], labels),
+                    in0=by_label(part[rt][:, halved], labels), scalar=0.5,
+                    in1=for_every_label(base[:, rt, :], labels), op0=ALU.mult, op1=ALU.add,
                 )
-                nc.sync.dma_start(
-                    out=out_0[rt].rearrange("p i j t e -> p (i j t e)")[
-                        :, h * (HALF // 2) : (h + 1) * (HALF // 2)
-                    ],
-                    in_=scale[rt][:],
+            for rt in row_tiles:
+                nc.vector.scalar_tensor_tensor(
+                    out=log_s[rt][:, cols], in0=log_s[rt][:, cols], scalar=0.5,
+                    in1=v2[rt][:, cols], op0=ALU.mult, op1=ALU.add,
                 )
+                stores.append(
+                    (out_2[rt].rearrange("p i j t e g -> p (i j t e g)")[:, cols], log_s[rt][:, cols])
+                )
+            return stores
+
+        def after_mean(acc, col0, width):
+            cols = slice(col0, col0 + width)
+            halved = slice(col0 // 2, (col0 + width) // 2)
+            labels = width // JTG
+            stores = []
+            add_bias_and_clip(diff, acc, 1, cols)
+            for rt in row_tiles:
+                nc.vector.tensor_tensor(
+                    out=by_label(diff[rt][:, cols], labels), in0=by_label(diff[rt][:, cols], labels),
+                    in1=for_every_label(m1[:, rt, :], labels), op=ALU.subtract,
+                )
+            for rt in row_tiles:
+                nc.scalar.activation(out=square[rt][:, cols], in_=diff[rt][:, cols], func=ACT.Square)
+            for rt in row_tiles:
+                nc.vector.tensor_tensor(
+                    out=mean[rt][:, cols], in0=diff[rt][:, cols], in1=s[rt][:, cols], op=ALU.mult
+                )
+            for rt in row_tiles:
+                nc.vector.tensor_tensor(
+                    out=by_label(mean[rt][:, cols], labels), in0=by_label(mean[rt][:, cols], labels),
+                    in1=for_every_label(m1[:, rt, :], labels), op=ALU.add,
+                )
+                stores.append(
+                    (out_1[rt].rearrange("p i j t e g -> p (i j t e g)")[:, cols], mean[rt][:, cols])
+                )
+            for rt in row_tiles:
+                nc.vector.tensor_tensor(
+                    out=square[rt][:, cols], in0=square[rt][:, cols], in1=inv_add[rt][:, cols],
+                    op=ALU.mult,
+                )
+            for rt in row_tiles:
+                nc.vector.tensor_tensor(
+                    out=scale[rt][:, halved], in0=pair(square[rt][:, cols], 0),
+                    in1=pair(square[rt][:, cols], 1), op=ALU.add,
+                )
+            for rt in row_tiles:
+                nc.vector.scalar_tensor_tensor(
+                    out=scale[rt][:, halved], in0=scale[rt][:, halved], scalar=-0.5,
+                    in1=part[rt][:, halved], op0=ALU.mult, op1=ALU.add,
+                )
+                stores.append(
+                    (out_0[rt].rearrange("p i j t e -> p (i j t e)")[:, halved], scale[rt][:, halved])
+                )
+            return stores
+
+        def finish(r, acc):
+            name, col0, width = ROUNDS[r]
+            if name == "v":
+                return after_log_std(acc, col0, width)
+            return after_mean(acc, col0, width)
+
+        last = len(ROUNDS) - 1
+        sums = [multiply(0)]
+        stores = []
+        for r in range(1, last + 1):
+            sums.append(multiply(r))
+            stores.extend(finish(r - 1, sums[r - 1]))
+        stores.extend(finish(last, sums[last]))
+        for where, result in stores:
+            nc.sync.dma_start(out=where, in_=result)

@@ -112,18 +112,6 @@ def tile_chainlveg_pa_k_kernel(
         nc.gpsimd.dma_start(out=mu_raw[:], in_=s_mu.rearrange("b p j e g -> p b (j e g)"))
         nc.gpsimd.dma_start(out=weight_raw[:], in_=s_weight.rearrange("b p j e -> p b (j e)"))
 
-        bias_all = keep.tile([P, 2, N], F32)
-        for w in range(2):
-            for h in range(N // BANK):
-                cols = slice(h * BANK, (h + 1) * BANK)
-                spread = psum.tile(
-                    [P, BANK], F32, name="spread", tag="bank%d" % (TRANSPOSE_BANKS + 2 * w + h)
-                )
-                nc.tensor.matmul(
-                    out=spread[:], lhsT=ones[:], rhs=bias_row[:, w, cols], start=True, stop=True
-                )
-                nc.scalar.copy(out=bias_all[:, w, cols], in_=spread[:])
-
         x_codes = keep.tile([P, PASSES, ROW_TILES * P], U32, align_bytes=64)
         x_planes = keep.tile([P, PASSES, ROW_TILES * P], U8, align_bytes=64)
 
@@ -157,6 +145,18 @@ def tile_chainlveg_pa_k_kernel(
                 quantise(g - 1, waiting)
             waiting = grouped
         quantise(PASSES - 1, waiting)
+
+        bias_all = keep.tile([P, 2, N], F32)
+        for w in range(2):
+            for h in range(N // BANK):
+                cols = slice(h * BANK, (h + 1) * BANK)
+                spread = psum.tile(
+                    [P, BANK], F32, name="spread", tag="bank%d" % (TRANSPOSE_BANKS + 2 * w + h)
+                )
+                nc.tensor.matmul(
+                    out=spread[:], lhsT=ones[:], rhs=bias_row[:, w, cols], start=True, stop=True
+                )
+                nc.scalar.copy(out=bias_all[:, w, cols], in_=spread[:])
 
         m1 = keep.tile([P, ROW_TILES, JTG], F32)
         v1 = keep.tile([P, ROW_TILES, JTG], F32)

@@ -35,11 +35,11 @@ ROUNDS = (("v", 0, 512), ("v", 512, 512), ("m", 0, 512), ("m", 512, 256), ("m", 
 FLOPS = 2 * ROW_TILES * P * K * 2 * N
 
 
-def load_scale_rows(nc, planes, scales, a):
+def load_scale_rows(queue, view, planes, scales, a):
     for quadrant in range(4):
-        nc.sync.dma_start(
-            out=planes[32 * quadrant : 32 * quadrant + 16, a, :].bitcast(I32),
-            in_=scales[SHARED * a : SHARED * (a + 1), 4 * quadrant : 4 * quadrant + 4, :].bitcast(I32),
+        queue.dma_start(
+            out=planes[32 * quadrant : 32 * quadrant + 16, a, :].bitcast(view),
+            in_=scales[SHARED * a : SHARED * (a + 1), 4 * quadrant : 4 * quadrant + 4, :].bitcast(view),
         )
 
 
@@ -111,6 +111,8 @@ def tile_chainlveg_pa_k_kernel(
         nc.gpsimd.dma_start(out=var_raw[:], in_=s_var.rearrange("b p j e g -> p b (j e g)"))
         nc.gpsimd.dma_start(out=mu_raw[:], in_=s_mu.rearrange("b p j e g -> p b (j e g)"))
         nc.gpsimd.dma_start(out=weight_raw[:], in_=s_weight.rearrange("b p j e -> p b (j e)"))
+        for a in range(PASSES // SHARED):
+            load_scale_rows(nc.gpsimd, F32, planes["m"], tcm_w_scales, a)
 
         x_codes = keep.tile([P, PASSES, ROW_TILES * P], U32, align_bytes=64)
         x_planes = keep.tile([P, PASSES, ROW_TILES * P], U8, align_bytes=64)
@@ -199,8 +201,8 @@ def tile_chainlveg_pa_k_kernel(
             ]
             per_load = LOAD_WORDS // width
             for first in range(0, PASSES, per_load):
-                if col0 == 0 and first % SHARED == 0:
-                    load_scale_rows(nc, planes[name], w_scales_dram, first // SHARED)
+                if name == "v" and col0 == 0 and first % SHARED == 0:
+                    load_scale_rows(nc.sync, I32, planes[name], w_scales_dram, first // SHARED)
                 w_words = ring.tile([P, per_load, width], U32, align_bytes=64, tag="w_words")
                 nc.sync.dma_start(
                     out=w_words[:].bitcast(I32),

@@ -108,6 +108,8 @@ def tile_chainlveg_pa_k_kernel(
         var_raw = keep.tile([P, ROW_TILES, 32], BF16)
         mu_raw = keep.tile([P, ROW_TILES, 32], BF16)
         weight_raw = keep.tile([P, ROW_TILES, 16], BF16)
+        for a in range(PASSES // SHARED):
+            load_scale_rows(nc.gpsimd, F32, planes["v"], tcv_w_scales, a)
         nc.gpsimd.dma_start(out=var_raw[:], in_=s_var.rearrange("b p j e g -> p b (j e g)"))
         nc.gpsimd.dma_start(out=mu_raw[:], in_=s_mu.rearrange("b p j e g -> p b (j e g)"))
         nc.gpsimd.dma_start(out=weight_raw[:], in_=s_weight.rearrange("b p j e -> p b (j e)"))
@@ -201,8 +203,6 @@ def tile_chainlveg_pa_k_kernel(
             ]
             per_load = LOAD_WORDS // width
             for first in range(0, PASSES, per_load):
-                if name == "v" and col0 == 0 and first % SHARED == 0:
-                    load_scale_rows(nc.sync, I32, planes[name], w_scales_dram, first // SHARED)
                 w_words = ring.tile([P, per_load, width], U32, align_bytes=64, tag="w_words")
                 nc.sync.dma_start(
                     out=w_words[:].bitcast(I32),

@@ -174,6 +174,13 @@ def tile_chainlveg_pa_k_kernel(
             )
         inv_e1 = keep.tile([P, ROW_TILES, JTG], F32)
         nc.scalar.activation(out=inv_e1[:], in_=v1[:], func=ACT.Exp, scale=-2.0)
+
+        unused = keep.tile([P, 1], F32)
+
+        def fetch_sigmoid_table():
+            nc.scalar.activation(out=unused[:], in_=ones[:, 0:1], func=ACT.Sigmoid)
+
+        fetch_sigmoid_table()
         var_pairs = var_raw[:].rearrange("p b (j g) -> p (b j) g", g=2)
         base_j = keep.tile([P, ROW_TILES * 16], F32)
         nc.vector.tensor_tensor(
@@ -262,6 +269,8 @@ def tile_chainlveg_pa_k_kernel(
                 )
             for rt in row_tiles:
                 nc.scalar.activation(out=log_s[rt][:, cols], in_=s[rt][:, cols], func=ACT.Ln)
+            if col0 + width < N:
+                fetch_sigmoid_table()
             for rt in row_tiles:
                 nc.vector.tensor_tensor(
                     out=by_label(inv_add[rt][:, cols], labels), in0=by_label(s[rt][:, cols], labels),

@@ -25,7 +25,7 @@ BANKS = 8
 JTG = 64
 SHARED = 4
 X_CHUNK = 4
-LOAD_WORDS = 1024
+LOAD_WORDS = 512
 TRANSPOSE_BANKS = 4
 CLIP = 1.0
 LOG_2PI = math.log(2.0 * math.pi)
@@ -77,7 +77,7 @@ def tile_chainlveg_pa_k_kernel(
         ctx.enter_context(tc.manual_schedule())
         keep = ctx.enter_context(tc.tile_pool(name="keep", bufs=1))
         stage = ctx.enter_context(tc.tile_pool(name="stage", bufs=3))
-        ring = ctx.enter_context(tc.tile_pool(name="ring", bufs=10))
+        ring = ctx.enter_context(tc.tile_pool(name="ring", bufs=20))
         psum = ctx.enter_context(tc.psum_pool(name="psum", bufs=1))
 
         bias_row = keep.tile([P, 2, N], BF16)

import math
from contextlib import ExitStack

import concourse.mybir as mybir
from concourse.masks import make_identity

F32 = mybir.dt.float32
BF16 = mybir.dt.bfloat16
I32 = mybir.dt.int32
U32 = mybir.dt.uint32
U8 = mybir.dt.uint8
FP8X4 = mybir.dt.float8_e4m3fn_x4
ALU = mybir.AluOpType
ACT = mybir.ActivationFunctionType

P = 128
PACK = 4
K_PASS = P * PACK
ROW_TILES = 2
K = 8192
PASSES = K // K_PASS
N = 1024
BANK = 512
BANKS = 8
JTG = 64
SHARED = 4
X_CHUNK = 4
LOAD_WORDS = 512
TRANSPOSE_BANKS = 4
CLIP = 1.0
LOG_2PI = math.log(2.0 * math.pi)

ROUNDS = (("v", 0, 512), ("v", 512, 512), ("m", 0, 512), ("m", 512, 256), ("m", 768, 256))

FLOPS = 2 * ROW_TILES * P * K * 2 * N


def load_scale_rows(queue, view, planes, scales, a):
    for quadrant in range(4):
        queue.dma_start(
            out=planes[32 * quadrant : 32 * quadrant + 16, a, :].bitcast(view),
            in_=scales[SHARED * a : SHARED * (a + 1), 4 * quadrant : 4 * quadrant + 4, :].bitcast(view),
        )


def by_label(full, labels):
    return full.rearrange("p (i c) -> p i c", i=labels)


def for_every_label(small, labels):
    return small.unsqueeze(1).to_broadcast([P, labels, small.shape[1]])


def pair(full, g):
    return full.rearrange("p (c g) -> p c g", g=2)[:, :, g]


def tile_chainlveg_pa_k_kernel(
    tc,
    x,
    s_weight,
    s_mu,
    s_var,
    tcm_w_words,
    tcm_w_scales,
    tcm_b,
    tcv_w_words,
    tcv_w_scales,
    tcv_b,
    out_0,
    out_1,
    out_2,
):
    nc = tc.nc
    row_tiles = range(ROW_TILES)
    with ExitStack() as ctx:
        ctx.enter_context(tc.manual_schedule())
        keep = ctx.enter_context(tc.tile_pool(name="keep", bufs=1))
        stage = ctx.enter_context(tc.tile_pool(name="stage", bufs=3))
        ring = ctx.enter_context(tc.tile_pool(name="ring", bufs=20))
        psum = ctx.enter_context(tc.psum_pool(name="psum", bufs=1))

        bias_row = keep.tile([P, 2, N], BF16)
        nc.vector.memset(bias_row[:].rearrange("p w n -> p (w n)").bitcast(I32), 0)
        ones = keep.tile([P, P], BF16)
        nc.vector.memset(ones[:], 1.0)
        planes = {}
        for name in ("v", "m"):
            planes[name] = keep.tile(
                [P, PASSES // SHARED, N], U8, align_bytes=64, name="planes_%s" % name
            )
            nc.vector.memset(planes[name][:].rearrange("p a n -> p (a n)").bitcast(I32), 0)
        ident = keep.tile([P, P], F32)
        make_identity(nc, ident[:])

        x_by_row = x.rearrange("b p k -> p b k")
        x_raw = []
        for c in range(PASSES // X_CHUNK):
            chunk = keep.tile([P, ROW_TILES, X_CHUNK * K_PASS], BF16, name="x_raw%d" % c)
            nc.sync.dma_start(
                out=chunk[:],
                in_=x_by_row[:, :, c * X_CHUNK * K_PASS : (c + 1) * X_CHUNK * K_PASS],
            )
            x_raw.append(chunk)

        nc.scalar.dma_start(out=bias_row[0:1, 0, :], in_=tcv_b.rearrange("(o n) -> o n", o=1))
        nc.scalar.dma_start(out=bias_row[0:1, 1, :], in_=tcm_b.rearrange("(o n) -> o n", o=1))
        var_raw = keep.tile([P, ROW_TILES, 32], BF16)
        mu_raw = keep.tile([P, ROW_TILES, 32], BF16)
        weight_raw = keep.tile([P, ROW_TILES, 16], BF16)
        for a in range(PASSES // SHARED):
            load_scale_rows(nc.gpsimd, F32, planes["v"], tcv_w_scales, a)
        nc.gpsimd.dma_start(out=var_raw[:], in_=s_var.rearrange("b p j e g -> p b (j e g)"))
        nc.gpsimd.dma_start(out=mu_raw[:], in_=s_mu.rearrange("b p j e g -> p b (j e g)"))
        nc.gpsimd.dma_start(out=weight_raw[:], in_=s_weight.rearrange("b p j e -> p b (j e)"))
        for a in range(PASSES // SHARED):
            load_scale_rows(nc.gpsimd, F32, planes["m"], tcm_w_scales, a)

        x_codes = keep.tile([P, PASSES, ROW_TILES * P], U32, align_bytes=64)
        x_planes = keep.tile([P, PASSES, ROW_TILES * P], U8, align_bytes=64)

        def quantise(g, grouped):
            nc.vector.quantize_mx(
                out=x_codes[:, g, :].bitcast(FP8X4), scales=x_planes[:, g, :], in_=grouped[:]
            )

        waiting = None
        for g in range(PASSES):
            c, g_in_chunk = divmod(g, X_CHUNK)
            flipped = psum.tile(
                [P, ROW_TILES, 2, P], F32, name="flipped", tag="bank%d" % (g % TRANSPOSE_BANKS)
            )
            for rt in row_tiles:
                words = x_raw[c][:, rt, :].bitcast(F32)
                first = g_in_chunk * (K_PASS // 2)
                for u in range(2):
                    nc.tensor.transpose(
                        flipped[:, rt, u, :],
                        words[:, first + u : first + K_PASS // 2 : 2],
                        ident[:],
                    )
            grouped = stage.tile([P, ROW_TILES * P * PACK], BF16, align_bytes=64)
            copy_out = nc.vector.tensor_copy if g % 4 == 3 else nc.scalar.copy
            copy_out(
                out=grouped[:].bitcast(F32).rearrange("p (a r u) -> p a r u", a=ROW_TILES, u=2),
                in_=flipped[:].rearrange("p a u r -> p a r u"),
            )
            if waiting is not None:
                quantise(g - 1, waiting)
            waiting = grouped
        quantise(PASSES - 1, waiting)

        bias_all = keep.tile([P, 2, N], F32)
        for w in range(2):
            for h in range(N // BANK):
                cols = slice(h * BANK, (h + 1) * BANK)
                spread = psum.tile(
                    [P, BANK], F32, name="spread", tag="bank%d" % (TRANSPOSE_BANKS + 2 * w + h)
                )
                nc.tensor.matmul(
                    out=spread[:], lhsT=ones[:], rhs=bias_row[:, w, cols], start=True, stop=True
                )
                nc.scalar.copy(out=bias_all[:, w, cols], in_=spread[:])

        m1 = keep.tile([P, ROW_TILES, JTG], F32)
        v1 = keep.tile([P, ROW_TILES, JTG], F32)
        for table, raw in ((v1, var_raw), (m1, mu_raw)):
            nc.vector.tensor_copy(
                out=table[:].rearrange("p b (j t g) -> p (b j) t g", t=2, g=2),
                in_=raw[:]
                .rearrange("p b (j g) -> p (b j) g", g=2)
                .unsqueeze(2)
                .to_broadcast([P, ROW_TILES * 16, 2, 2]),
            )
        inv_e1 = keep.tile([P, ROW_TILES, JTG], F32)
        nc.scalar.activation(out=inv_e1[:], in_=v1[:], func=ACT.Exp, scale=-2.0)

        unused = keep.tile([P, 1], F32)

        def fetch_sigmoid_table():
            nc.scalar.activation(out=unused[:], in_=ones[:, 0:1], func=ACT.Sigmoid)

        fetch_sigmoid_table()
        var_pairs = var_raw[:].rearrange("p b (j g) -> p (b j) g", g=2)
        base_j = keep.tile([P, ROW_TILES * 16], F32)
        nc.vector.tensor_tensor(
            out=base_j[:], in0=var_pairs[:, :, 0], in1=var_pairs[:, :, 1], op=ALU.add
        )
        nc.vector.tensor_tensor(
            out=base_j[:], in0=weight_raw[:].rearrange("p b j -> p (b j)"), in1=base_j[:], op=ALU.subtract
        )
        base = keep.tile([P, ROW_TILES, JTG // 2], F32)
        nc.vector.tensor_scalar(
            out=base[:].rearrange("p b (j t) -> p (b j) t", t=2),
            in0=base_j[:].unsqueeze(2).to_broadcast([P, ROW_TILES * 16, 2]),
            scalar1=-LOG_2PI,
            scalar2=None,
            op0=ALU.add,
        )

        weights = {"v": (tcv_w_words, tcv_w_scales), "m": (tcm_w_words, tcm_w_scales)}

        def multiply(r):
            name, col0, width = ROUNDS[r]
            w_words_dram, w_scales_dram = weights[name]
            cols = slice(col0, col0 + width)
            acc = [
                psum.tile([P, width], F32, name="acc", tag="bank%d" % ((2 * r + rt) % BANKS))
                for rt in row_tiles
            ]
            per_load = LOAD_WORDS // width
            for first in range(0, PASSES, per_load):
                w_words = ring.tile([P, per_load, width], U32, align_bytes=64, tag="w_words")
                nc.sync.dma_start(
                    out=w_words[:].bitcast(I32),
                    in_=w_words_dram[first : first + per_load, :, cols, :]
                    .rearrange("g p n t -> p g (n t)")
                    .bitcast(I32),
                )
                for g in range(first, first + per_load):
                    for rt in row_tiles:
                        rows = slice(rt * P, (rt + 1) * P)
                        nc.tensor.matmul_mx(
                            out=acc[rt][:],
                            lhsT=x_codes[:, g, rows].bitcast(FP8X4),
                            lhsT_scale=x_planes[:, g, rows],
                            rhs=w_words[:, g - first, :].bitcast(FP8X4),
                            rhs_scale=planes[name][4 * (g % SHARED) : P, g // SHARED, cols],
                            start=(g == 0),
                            stop=(g == PASSES - 1),
                        )
            return acc

        v2 = [keep.tile([P, N], F32, name="v2_%d" % rt) for rt in row_tiles]
        s = [keep.tile([P, N], F32, name="s_%d" % rt) for rt in row_tiles]
        log_s = [keep.tile([P, N], F32, name="log_s_%d" % rt) for rt in row_tiles]
        inv_add = [keep.tile([P, N], F32, name="inv_add_%d" % rt) for rt in row_tiles]
        part = [keep.tile([P, N // 2], F32, name="part_%d" % rt) for rt in row_tiles]
        diff = [keep.tile([P, N], F32, name="diff_%d" % rt) for rt in row_tiles]
        square = [keep.tile([P, N], F32, name="square_%d" % rt) for rt in row_tiles]
        mean = [keep.tile([P, N], F32, name="mean_%d" % rt) for rt in row_tiles]
        scale = [keep.tile([P, N // 2], F32, name="scale_%d" % rt) for rt in row_tiles]

        def add_bias_and_clip(dst, acc, w, cols):
            for rt in row_tiles:
                nc.vector.tensor_tensor(
                    out=dst[rt][:, cols], in0=acc[rt][:], in1=bias_all[:, w, cols], op=ALU.add
                )
            for rt in row_tiles:
                nc.vector.tensor_scalar(
                    out=dst[rt][:, cols], in0=dst[rt][:, cols],
                    scalar1=-CLIP, scalar2=CLIP, op0=ALU.max, op1=ALU.min,
                )

        def after_log_std(acc, col0, width):
            cols = slice(col0, col0 + width)
            halved = slice(col0 // 2, (col0 + width) // 2)
            labels = width // JTG
            stores = []
            add_bias_and_clip(v2, acc, 0, cols)
            for rt in row_tiles:
                nc.vector.tensor_tensor(
                    out=by_label(s[rt][:, cols], labels), in0=by_label(v2[rt][:, cols], labels),
                    in1=for_every_label(v1[:, rt, :], labels), op=ALU.subtract,
                )
            for rt in row_tiles:
                nc.scalar.activation(
                    out=s[rt][:, cols], in_=s[rt][:, cols], func=ACT.Sigmoid, scale=-2.0
                )
            for rt in row_tiles:
                nc.scalar.activation(out=log_s[rt][:, cols], in_=s[rt][:, cols], func=ACT.Ln)
            if col0 + width < N:
                fetch_sigmoid_table()
            for rt in row_tiles:
                nc.vector.tensor_tensor(
                    out=by_label(inv_add[rt][:, cols], labels), in0=by_label(s[rt][:, cols], labels),
                    in1=for_every_label(inv_e1[:, rt, :], labels), op=ALU.mult,
                )
            for rt in row_tiles:
                nc.vector.tensor_tensor(
                    out=part[rt][:, halved], in0=pair(log_s[rt][:, cols], 0),
                    in1=pair(log_s[rt][:, cols], 1), op=ALU.add,
                )
            for rt in row_tiles:
                nc.vector.scalar_tensor_tensor(
                    out=by_label(part[rt][:, halved], labels),
                    in0=by_label(part[rt][:, halved], labels), scalar=0.5,
                    in1=for_every_label(base[:, rt, :], labels), op0=ALU.mult, op1=ALU.add,
                )
            for rt in row_tiles:
                nc.vector.scalar_tensor_tensor(
                    out=log_s[rt][:, cols], in0=log_s[rt][:, cols], scalar=0.5,
                    in1=v2[rt][:, cols], op0=ALU.mult, op1=ALU.add,
                )
                stores.append(
                    (out_2[rt].rearrange("p i j t e g -> p (i j t e g)")[:, cols], log_s[rt][:, cols])
                )
            return stores

        def after_mean(acc, col0, width):
            cols = slice(col0, col0 + width)
            halved = slice(col0 // 2, (col0 + width) // 2)
            labels = width // JTG
            stores = []
            add_bias_and_clip(diff, acc, 1, cols)
            for rt in row_tiles:
                nc.vector.tensor_tensor(
                    out=by_label(diff[rt][:, cols], labels), in0=by_label(diff[rt][:, cols], labels),
                    in1=for_every_label(m1[:, rt, :], labels), op=ALU.subtract,
                )
            for rt in row_tiles:
                nc.scalar.activation(out=square[rt][:, cols], in_=diff[rt][:, cols], func=ACT.Square)
            for rt in row_tiles:
                nc.vector.tensor_tensor(
                    out=mean[rt][:, cols], in0=diff[rt][:, cols], in1=s[rt][:, cols], op=ALU.mult
                )
            for rt in row_tiles:
                nc.vector.tensor_tensor(
                    out=by_label(mean[rt][:, cols], labels), in0=by_label(mean[rt][:, cols], labels),
                    in1=for_every_label(m1[:, rt, :], labels), op=ALU.add,
                )
                stores.append(
                    (out_1[rt].rearrange("p i j t e g -> p (i j t e g)")[:, cols], mean[rt][:, cols])
                )
            for rt in row_tiles:
                nc.vector.tensor_tensor(
                    out=square[rt][:, cols], in0=square[rt][:, cols], in1=inv_add[rt][:, cols],
                    op=ALU.mult,
                )
            for rt in row_tiles:
                nc.vector.tensor_tensor(
                    out=scale[rt][:, halved], in0=pair(square[rt][:, cols], 0),
                    in1=pair(square[rt][:, cols], 1), op=ALU.add,
                )
            for rt in row_tiles:
                nc.vector.scalar_tensor_tensor(
                    out=scale[rt][:, halved], in0=scale[rt][:, halved], scalar=-0.5,
                    in1=part[rt][:, halved], op0=ALU.mult, op1=ALU.add,
                )
                stores.append(
                    (out_0[rt].rearrange("p i j t e -> p (i j t e)")[:, halved], scale[rt][:, halved])
                )
            return stores

        def finish(r, acc):
            name, col0, width = ROUNDS[r]
            if name == "v":
                return after_log_std(acc, col0, width)
            return after_mean(acc, col0, width)

        last = len(ROUNDS) - 1
        sums = [multiply(0)]
        stores = []
        for r in range(1, last + 1):
            sums.append(multiply(r))
            stores.extend(finish(r - 1, sums[r - 1]))
        stores.extend(finish(last, sums[last]))
        for where, result in stores:
            nc.sync.dma_start(out=where, in_=result)
